import numpy as np
import ml_dtypes


def mxq(x, axis, fmt="e4m3"):
    dtype, down = {"e4m3": (ml_dtypes.float8_e4m3fn, 7), "e5m2": (ml_dtypes.float8_e5m2, 14)}[fmt]
    v = np.moveaxis(np.asarray(x, np.float32).astype(ml_dtypes.bfloat16).astype(np.float64), axis, -1)
    blocks = v.reshape(v.shape[:-1] + (-1, 32))
    amax = np.abs(blocks).max(-1, keepdims=True)
    byte = np.maximum(np.where(amax > 0, np.frexp(amax)[1] - 1 + 127, 0) - down, 1)
    scale = np.exp2(byte - 127.0)
    codes = (blocks / scale).astype(np.float32).astype(dtype).astype(np.float64)
    return np.moveaxis((codes * scale).reshape(v.shape), -1, axis)


WIDE = False


def mx_kscale(k):
    if not WIDE:
        return np.ones(k)
    levels = np.array([10, -10, 5, -5, 0])
    if k % 512:
        return np.exp2(np.random.permutation(np.resize(levels, k // 32))).repeat(32)
    a = np.empty((k // 512, 16))
    for p in range(k // 512):
        a[p, :8] = np.random.permutation(np.resize(levels, 8))
        for g in range(8):
            far = levels[np.abs(levels - a[p, g]) >= 10]
            a[p, g + 8] = far[np.random.randint(len(far))]
    return np.exp2(a.ravel()).repeat(32)


BF16 = ml_dtypes.bfloat16


def bf(x):
    return np.asarray(x, np.float32).astype(BF16)


def f64(x):
    return np.asarray(x).astype(np.float64)


BATCH, IN_DIM, OUT_DIM = 4096, 512, 1024


def setup_inputs():
    s = mx_kscale(IN_DIM)
    a = np.round(np.log2(s))
    x = np.random.standard_normal((BATCH, IN_DIM)) * (8.0 / np.sqrt(IN_DIM)) * s
    shift = np.round(np.random.uniform(-10.0, -1.0, (IN_DIM, OUT_DIM))) - a[:, None]
    sign = np.round(np.random.uniform(0.0, 1.0, (IN_DIM, OUT_DIM)))
    bias = np.random.standard_normal((1, OUT_DIM)) * 0.5
    return {"x": bf(x), "shift": bf(shift), "sign": bf(sign), "bias": bf(bias)}


def reference(x, shift, sign, bias):
    W = np.exp2(f64(shift)) * np.power(-1.0, f64(sign))
    return (mxq(f64(x), 1, "e4m3") @ mxq(W, 0, "e4m3")) + f64(bias)

@@ -1,0 +1,180 @@
+from contextlib import ExitStack
+
+import concourse.mybir as mybir
+from concourse.masks import make_identity
+
+F32 = mybir.dt.float32
+BF16 = mybir.dt.bfloat16
+U32 = mybir.dt.uint32
+U8 = mybir.dt.uint8
+FP8X4 = mybir.dt.float8_e4m3fn_x4
+ALU = mybir.AluOpType
+ACT = mybir.ActivationFunctionType
+
+P = 128
+BATCH, K, OUT = 4096, 512, 1024
+PACK = 4
+TILES = BATCH // P
+GROUP = 4
+GROUPS = TILES // GROUP
+HALF = 512
+WORDS = K // 2
+FLOPS = 2 * BATCH * K * OUT
+LN2 = 0.6931471805599453
+
+X_CHUNKS = ((0, 4), (4, 8), (8, 16), (16, 24), (24, 32))
+SCALAR_SHARE = ((2, 4, 6), (0, 3, 6)) + ((0, 4),) * (GROUPS - 2)
+STORE_CUTS = (((0, 1), (1, 2), (2, 3), (3, 4)), ((0, 2), (2, 4))) + (((0, 4),),) * (GROUPS - 2)
+QUANT_AFTER = 2
+OUT_BUFS = 5
+
+
+def tile_denseshift_t_kernel(tc, x, shift, sign, bias, out):
+    nc = tc.nc
+    with ExitStack() as ctx:
+        ctx.enter_context(tc.manual_schedule())
+        keep = ctx.enter_context(tc.tile_pool(name="keep", bufs=1))
+        stage = ctx.enter_context(tc.tile_pool(name="stage", bufs=3))
+        results = ctx.enter_context(tc.tile_pool(name="results", bufs=OUT_BUFS))
+        psum_t = ctx.enter_context(tc.psum_pool(name="psum_t", bufs=2))
+        psum_acc = ctx.enter_context(tc.psum_pool(name="psum_acc", bufs=6))
+
+        warm = keep.tile([P, 1], F32, name="warm")
+        ones = keep.tile([P, P], BF16, name="ones")
+        ident = keep.tile([P, P], F32, name="ident")
+        bias_pad = keep.tile([P, OUT], BF16, name="bias_pad")
+        bias_sb = keep.tile([P, OUT], F32, name="bias_sb")
+        x_sb = keep.tile([P, TILES * K], BF16, name="x_sb")
+        shift_sb = keep.tile([P, PACK * OUT], BF16, name="shift_sb")
+        sign_sb = keep.tile([P, PACK * OUT], BF16, name="sign_sb")
+        pow_g = keep.tile([P, OUT * PACK], BF16, name="pow_g")
+        sgn_g = keep.tile([P, OUT * PACK], BF16, name="sgn_g")
+        w_g = keep.tile([P, OUT * PACK], BF16, name="w_g", align_bytes=64)
+        w_codes = keep.tile([P, OUT], U32, name="w_codes", align_bytes=64)
+        w_scales = keep.tile([P, OUT], U8, name="w_scales", align_bytes=64)
+        x_codes = keep.tile([P, BATCH], U32, name="x_codes", align_bytes=64)
+        x_scales = keep.tile([P, BATCH], U8, name="x_scales", align_bytes=64)
+
+        nc.vector.memset(bias_pad[:], 0.0)
+        nc.vector.memset(ones[:], 1.0)
+        nc.vector.memset(warm[:], 0.0)
+        make_identity(nc, ident[:])
+
+        for dst, src in ((shift_sb, shift), (sign_sb, sign)):
+            nc.sync.dma_start(
+                out=dst[:],
+                in_=src.rearrange("(q t) o -> q (t o)", t=PACK),
+            )
+            if dst is shift_sb:
+                nc.sync.dma_start(out=bias_pad[0:1, :], in_=bias)
+        x_rows = x.rearrange("(p i) k -> p (i k)", i=TILES)
+        for first, last in X_CHUNKS:
+            nc.sync.dma_start(out=x_sb[:, first * K : last * K], in_=x_rows[:, first * K : last * K])
+        x_words = x_sb[:].bitcast(F32)
+        out_rows = out.rearrange("(p i) o -> p i o", i=TILES)
+
+        nc.scalar.activation(out=warm[:], in_=warm[:], func=ACT.Exp)
+
+        spreads = []
+        for h in range(2):
+            spread = psum_acc.tile([P, HALF], F32, tag="acc", name="spread")
+            nc.tensor.matmul(
+                out=spread[:], lhsT=ones[:], rhs=bias_pad[:, h * HALF : (h + 1) * HALF], start=True, stop=True
+            )
+            spreads.append(spread)
+
+        def rows_view(t, h):
+            by_row = t[:].rearrange("q (t o) -> q t o", t=PACK)[:, :, h * HALF : (h + 1) * HALF]
+            return by_row.rearrange("q t (c i) -> q c t i", i=4)
+
+        def grouped_view(t, h):
+            part = t[:, h * HALF * PACK : (h + 1) * HALF * PACK]
+            return part.rearrange("q (c i t) -> q c t i", i=4, t=PACK)
+
+        def power(h):
+            nc.scalar.activation(
+                out=grouped_view(pow_g, h), in_=rows_view(shift_sb, h), func=ACT.Exp, scale=LN2
+            )
+
+        def plus_minus(h):
+            nc.vector.tensor_scalar(
+                out=grouped_view(sgn_g, h), in0=rows_view(sign_sb, h),
+                scalar1=-2.0, scalar2=1.0, op0=ALU.mult, op1=ALU.add,
+            )
+
+        def weights(h):
+            part = slice(h * HALF * PACK, (h + 1) * HALF * PACK)
+            nc.vector.tensor_tensor(out=w_g[:, part], in0=pow_g[:, part], in1=sgn_g[:, part], op=ALU.mult)
+
+        def quantise_w(h):
+            cols = slice(h * HALF, (h + 1) * HALF)
+            nc.vector.quantize_mx(
+                out=w_codes[:, cols].bitcast(FP8X4),
+                scales=w_scales[:, cols],
+                in_=w_g[:, h * HALF * PACK : (h + 1) * HALF * PACK],
+            )
+
+        def transpose_group(g):
+            x_g = stage.tile([P, GROUP * K], BF16, tag="x_g", name="x_g", align_bytes=64)
+            x_g_words = x_g[:].bitcast(F32)
+            for b in range(2):
+                xt = psum_t.tile([P, 4, P], F32, tag="xt", name="xt")
+                for pair in range(2):
+                    i = GROUP * g + 2 * b + pair
+                    for u in range(2):
+                        every_second = slice(WORDS * i + u, WORDS * (i + 1), 2)
+                        nc.tensor.transpose(xt[:, 2 * pair + u, :], x_words[:, every_second], ident[:])
+                nc.scalar.copy(
+                    out=x_g_words[:, 2 * WORDS * b : 2 * WORDS * (b + 1)].rearrange(
+                        "q (pair r u) -> q pair r u", pair=2, u=2
+                    ),
+                    in_=xt[:].rearrange("q (pair u) r -> q pair r u", u=2),
+                )
+            return x_g
+
+        def quantise_x(g, x_g):
+            cols = slice(g * GROUP * P, (g + 1) * GROUP * P)
+            nc.vector.quantize_mx(out=x_codes[:, cols].bitcast(FP8X4), scales=x_scales[:, cols], in_=x_g[:])
+
+        power(0)
+        power(1)
+        plus_minus(0)
+        weights(0)
+        plus_minus(1)
+        quantise_w(0)
+        weights(1)
+        x_first = transpose_group(0)
+        for h in range(2):
+            nc.scalar.copy(out=bias_sb[:, h * HALF : (h + 1) * HALF], in_=spreads[h][:])
+        quantise_x(0, x_first)
+        quantise_w(1)
+
+        for g in range(GROUPS):
+            x_next = transpose_group(g + 1) if g + 1 < GROUPS else None
+            o_sb = results.tile([P, GROUP, OUT], F32, tag="o_sb", name="o_sb")
+            for j in range(2 * GROUP):
+                t, h = divmod(j, 2)
+                rows = slice((GROUP * g + t) * P, (GROUP * g + t + 1) * P)
+                cols = slice(h * HALF, (h + 1) * HALF)
+                acc = psum_acc.tile([P, HALF], F32, tag="acc", name="acc")
+                nc.tensor.matmul_mx(
+                    out=acc[:],
+                    lhsT=x_codes[:, rows].bitcast(FP8X4),
+                    lhsT_scale=x_scales[:, rows],
+                    rhs=w_codes[:, cols].bitcast(FP8X4),
+                    rhs_scale=w_scales[:, cols],
+                    start=True,
+                    stop=True,
+                )
+                if j in SCALAR_SHARE[g]:
+                    nc.scalar.copy(out=o_sb[:, t, cols], in_=acc[:])
+                    nc.gpsimd.tensor_tensor(out=o_sb[:, t, cols], in0=o_sb[:, t, cols], in1=bias_sb[:, cols], op=ALU.add)
+                else:
+                    nc.vector.tensor_tensor(out=o_sb[:, t, cols], in0=acc[:], in1=bias_sb[:, cols], op=ALU.add)
+                if j == QUANT_AFTER and x_next is not None:
+                    quantise_x(g + 1, x_next)
+                for first, last in STORE_CUTS[g]:
+                    if j == 2 * last - 1:
+                        nc.sync.dma_start(
+                            out=out_rows[:, GROUP * g + first : GROUP * g + last, :], in_=o_sb[:, first:last, :]
+                        )

@@ -22,9 +22,10 @@ WORDS = K // 2
 FLOPS = 2 * BATCH * K * OUT
 LN2 = 0.6931471805599453
 
+QUARTER = 256
 X_CHUNKS = ((0, 4), (4, 8), (8, 16), (16, 24), (24, 32))
-SCALAR_SHARE = ((2, 4, 6), (0, 3, 6)) + ((0, 4),) * (GROUPS - 2)
-STORE_CUTS = (((0, 1), (1, 2), (2, 3), (3, 4)), ((0, 2), (2, 4))) + (((0, 4),),) * (GROUPS - 2)
+SCALAR_SHARE = (None, (0, 3, 6)) + ((0, 4),) * (GROUPS - 2)
+STORE_CUTS = (None, ((0, 2), (2, 4))) + (((0, 4),),) * (GROUPS - 2)
 QUANT_AFTER = 2
 OUT_BUFS = 5
 
@@ -60,12 +61,9 @@ def tile_denseshift_t_kernel(tc, x, shift, sign, bias, out):
         nc.vector.memset(warm[:], 0.0)
         make_identity(nc, ident[:])
 
-        for dst, src in ((shift_sb, shift), (sign_sb, sign)):
-            nc.sync.dma_start(
-                out=dst[:],
-                in_=src.rearrange("(q t) o -> q (t o)", t=PACK),
-            )
-            if dst is shift_sb:
+        for dst, src in ((sign_sb, sign), (shift_sb, shift)):
+            nc.sync.dma_start(out=dst[:], in_=src.rearrange("(q t) o -> q (t o)", t=PACK))
+            if dst is sign_sb:
                 nc.sync.dma_start(out=bias_pad[0:1, :], in_=bias)
         x_rows = x.rearrange("(p i) k -> p (i k)", i=TILES)
         for first, last in X_CHUNKS:
@@ -75,106 +73,150 @@ def tile_denseshift_t_kernel(tc, x, shift, sign, bias, out):
 
         nc.scalar.activation(out=warm[:], in_=warm[:], func=ACT.Exp)
 
-        spreads = []
-        for h in range(2):
-            spread = psum_acc.tile([P, HALF], F32, tag="acc", name="spread")
-            nc.tensor.matmul(
-                out=spread[:], lhsT=ones[:], rhs=bias_pad[:, h * HALF : (h + 1) * HALF], start=True, stop=True
-            )
-            spreads.append(spread)
-
-        def rows_view(t, h):
-            by_row = t[:].rearrange("q (t o) -> q t o", t=PACK)[:, :, h * HALF : (h + 1) * HALF]
+        def rows_view(t, cols):
+            by_row = t[:].rearrange("q (t o) -> q t o", t=PACK)[:, :, cols]
             return by_row.rearrange("q t (c i) -> q c t i", i=4)
 
-        def grouped_view(t, h):
-            part = t[:, h * HALF * PACK : (h + 1) * HALF * PACK]
-            return part.rearrange("q (c i t) -> q c t i", i=4, t=PACK)
+        def grouped(cols):
+            return slice(cols.start * PACK, cols.stop * PACK)
 
-        def power(h):
+        def grouped_view(t, cols):
+            return t[:, grouped(cols)].rearrange("q (c i t) -> q c t i", i=4, t=PACK)
+
+        def half(h):
+            return slice(h * HALF, (h + 1) * HALF)
+
+        def quarter(i):
+            return slice(i * QUARTER, (i + 1) * QUARTER)
+
+        def power(cols):
             nc.scalar.activation(
-                out=grouped_view(pow_g, h), in_=rows_view(shift_sb, h), func=ACT.Exp, scale=LN2
+                out=grouped_view(pow_g, cols), in_=rows_view(shift_sb, cols), func=ACT.Exp, scale=LN2
             )
 
-        def plus_minus(h):
+        def plus_minus(cols):
             nc.vector.tensor_scalar(
-                out=grouped_view(sgn_g, h), in0=rows_view(sign_sb, h),
+                out=grouped_view(sgn_g, cols), in0=rows_view(sign_sb, cols),
                 scalar1=-2.0, scalar2=1.0, op0=ALU.mult, op1=ALU.add,
             )
 
-        def weights(h):
-            part = slice(h * HALF * PACK, (h + 1) * HALF * PACK)
+        def weights(cols):
+            part = grouped(cols)
             nc.vector.tensor_tensor(out=w_g[:, part], in0=pow_g[:, part], in1=sgn_g[:, part], op=ALU.mult)
 
-        def quantise_w(h):
-            cols = slice(h * HALF, (h + 1) * HALF)
+        def quantise_w(cols):
             nc.vector.quantize_mx(
-                out=w_codes[:, cols].bitcast(FP8X4),
-                scales=w_scales[:, cols],
-                in_=w_g[:, h * HALF * PACK : (h + 1) * HALF * PACK],
+                out=w_codes[:, cols].bitcast(FP8X4), scales=w_scales[:, cols], in_=w_g[:, grouped(cols)]
             )
 
-        def transpose_group(g):
-            x_g = stage.tile([P, GROUP * K], BF16, tag="x_g", name="x_g", align_bytes=64)
+        def new_x_group():
+            return stage.tile([P, GROUP * K], BF16, tag="x_g", name="x_g", align_bytes=64)
+
+        def transpose_pair(g, b):
+            xt = psum_t.tile([P, 4, P], F32, tag="xt", name="xt")
+            for pair in range(2):
+                i = GROUP * g + 2 * b + pair
+                for u in range(2):
+                    every_second = slice(WORDS * i + u, WORDS * (i + 1), 2)
+                    nc.tensor.transpose(xt[:, 2 * pair + u, :], x_words[:, every_second], ident[:])
+            return xt
+
+        def copy_pair(copy, xt, x_g, b):
             x_g_words = x_g[:].bitcast(F32)
-            for b in range(2):
-                xt = psum_t.tile([P, 4, P], F32, tag="xt", name="xt")
-                for pair in range(2):
-                    i = GROUP * g + 2 * b + pair
-                    for u in range(2):
-                        every_second = slice(WORDS * i + u, WORDS * (i + 1), 2)
-                        nc.tensor.transpose(xt[:, 2 * pair + u, :], x_words[:, every_second], ident[:])
-                nc.scalar.copy(
-                    out=x_g_words[:, 2 * WORDS * b : 2 * WORDS * (b + 1)].rearrange(
-                        "q (pair r u) -> q pair r u", pair=2, u=2
-                    ),
-                    in_=xt[:].rearrange("q (pair u) r -> q pair r u", u=2),
-                )
-            return x_g
+            copy(
+                out=x_g_words[:, 2 * WORDS * b : 2 * WORDS * (b + 1)].rearrange(
+                    "q (pair r u) -> q pair r u", pair=2, u=2
+                ),
+                in_=xt[:].rearrange("q (pair u) r -> q pair r u", u=2),
+            )
 
         def quantise_x(g, x_g):
             cols = slice(g * GROUP * P, (g + 1) * GROUP * P)
             nc.vector.quantize_mx(out=x_codes[:, cols].bitcast(FP8X4), scales=x_scales[:, cols], in_=x_g[:])
 
-        power(0)
-        power(1)
-        plus_minus(0)
-        weights(0)
-        plus_minus(1)
-        quantise_w(0)
-        weights(1)
-        x_first = transpose_group(0)
-        for h in range(2):
-            nc.scalar.copy(out=bias_sb[:, h * HALF : (h + 1) * HALF], in_=spreads[h][:])
-        quantise_x(0, x_first)
-        quantise_w(1)
+        def multiply(g, t, h):
+            rows = slice((GROUP * g + t) * P, (GROUP * g + t + 1) * P)
+            cols = half(h)
+            acc = psum_acc.tile([P, HALF], F32, tag="acc", name="acc")
+            nc.tensor.matmul_mx(
+                out=acc[:],
+                lhsT=x_codes[:, rows].bitcast(FP8X4),
+                lhsT_scale=x_scales[:, rows],
+                rhs=w_codes[:, cols].bitcast(FP8X4),
+                rhs_scale=w_scales[:, cols],
+                start=True,
+                stop=True,
+            )
+            return acc
 
-        for g in range(GROUPS):
-            x_next = transpose_group(g + 1) if g + 1 < GROUPS else None
+        def add_on_vector(o_sb, acc, t, h):
+            nc.vector.tensor_tensor(out=o_sb[:, t, half(h)], in0=acc[:], in1=bias_sb[:, half(h)], op=ALU.add)
+
+        def add_on_gpsimd(o_sb, acc, t, h):
+            part = o_sb[:, t, half(h)]
+            nc.scalar.copy(out=part, in_=acc[:])
+            nc.gpsimd.tensor_tensor(out=part, in0=part, in1=bias_sb[:, half(h)], op=ALU.add)
+
+        def store(o_sb, g, first, last):
+            nc.sync.dma_start(
+                out=out_rows[:, GROUP * g + first : GROUP * g + last, :], in_=o_sb[:, first:last, :]
+            )
+
+        for h in range(2):
+            spread = psum_acc.tile([P, HALF], F32, tag="acc", name="acc")
+            nc.tensor.matmul(out=spread[:], lhsT=ones[:], rhs=bias_pad[:, half(h)], start=True, stop=True)
+            nc.scalar.copy(out=bias_sb[:, half(h)], in_=spread[:])
+
+        plus_minus(half(0))
+        plus_minus(half(1))
+        for i in range(4):
+            power(quarter(i))
+        x_g = new_x_group()
+        for i in range(2):
+            xt = transpose_pair(0, i)
+            weights(quarter(i))
+            copy_pair(nc.vector.tensor_copy, xt, x_g, i)
+        quantise_w(half(0))
+        weights(quarter(2))
+        quantise_x(0, x_g)
+        weights(quarter(3))
+        quantise_w(quarter(2))
+        quantise_w(quarter(3))
+
+        x_next = new_x_group()
+        ahead = [transpose_pair(1, b) for b in range(2)]
+        o_sb = results.tile([P, GROUP, OUT], F32, tag="o_sb", name="o_sb")
+        firsts = [multiply(0, t, 0) for t in range(GROUP)]
+        for t in range(3):
+            add_on_gpsimd(o_sb, firsts[t], t, 0)
+        for b in range(2):
+            copy_pair(nc.scalar.copy, ahead[b], x_next, b)
+        add_on_vector(o_sb, firsts[3], 3, 0)
+        for t in range(GROUP):
+            acc = multiply(0, t, 1)
+            add_on_vector(o_sb, acc, t, 1)
+            if t == 1:
+                quantise_x(1, x_next)
+            if t < 2:
+                store(o_sb, 0, t, t + 1)
+        store(o_sb, 0, 2, 4)
+
+        for g in range(1, GROUPS):
+            x_next = None
+            if g + 1 < GROUPS:
+                x_next = new_x_group()
+                for b in range(2):
+                    copy_pair(nc.scalar.copy, transpose_pair(g + 1, b), x_next, b)
             o_sb = results.tile([P, GROUP, OUT], F32, tag="o_sb", name="o_sb")
             for j in range(2 * GROUP):
                 t, h = divmod(j, 2)
-                rows = slice((GROUP * g + t) * P, (GROUP * g + t + 1) * P)
-                cols = slice(h * HALF, (h + 1) * HALF)
-                acc = psum_acc.tile([P, HALF], F32, tag="acc", name="acc")
-                nc.tensor.matmul_mx(
-                    out=acc[:],
-                    lhsT=x_codes[:, rows].bitcast(FP8X4),
-                    lhsT_scale=x_scales[:, rows],
-                    rhs=w_codes[:, cols].bitcast(FP8X4),
-                    rhs_scale=w_scales[:, cols],
-                    start=True,
-                    stop=True,
-                )
+                acc = multiply(g, t, h)
                 if j in SCALAR_SHARE[g]:
-                    nc.scalar.copy(out=o_sb[:, t, cols], in_=acc[:])
-                    nc.gpsimd.tensor_tensor(out=o_sb[:, t, cols], in0=o_sb[:, t, cols], in1=bias_sb[:, cols], op=ALU.add)
+                    add_on_gpsimd(o_sb, acc, t, h)
                 else:
-                    nc.vector.tensor_tensor(out=o_sb[:, t, cols], in0=acc[:], in1=bias_sb[:, cols], op=ALU.add)
+                    add_on_vector(o_sb, acc, t, h)
                 if j == QUANT_AFTER and x_next is not None:
                     quantise_x(g + 1, x_next)
                 for first, last in STORE_CUTS[g]:
                     if j == 2 * last - 1:
-                        nc.sync.dma_start(
-                            out=out_rows[:, GROUP * g + first : GROUP * g + last, :], in_=o_sb[:, first:last, :]
-                        )
+                        store(o_sb, g, first, last)

@@ -24,9 +24,15 @@ LN2 = 0.6931471805599453
 
 QUARTER = 256
 X_CHUNKS = ((0, 4), (4, 8), (8, 16), (16, 24), (24, 32))
-SCALAR_SHARE = (None, (0, 3, 6)) + ((0, 4),) * (GROUPS - 2)
-STORE_CUTS = (None, ((0, 2), (2, 4))) + (((0, 4),),) * (GROUPS - 2)
-QUANT_AFTER = 2
+STORE_CUTS = (((0, 1), (1, 2), (2, 4)),) + (((0, 2), (2, 4)),) * (GROUPS - 1)
+QUANT_AFTER = 3
+S_BANKS = (0, 1)
+T_AFTER = 2
+S_BUFS = 2
+S0 = (2, 3)
+V0 = ((0, 0), (0, 1), (1, 0), (1, 1), (2, 1), (3, 1))
+Q0 = 1
+V_BUFS = 4
 OUT_BUFS = 5
 
 
@@ -38,7 +44,8 @@ def tile_denseshift_t_kernel(tc, x, shift, sign, bias, out):
         stage = ctx.enter_context(tc.tile_pool(name="stage", bufs=3))
         results = ctx.enter_context(tc.tile_pool(name="results", bufs=OUT_BUFS))
         psum_t = ctx.enter_context(tc.psum_pool(name="psum_t", bufs=2))
-        psum_acc = ctx.enter_context(tc.psum_pool(name="psum_acc", bufs=6))
+        psum_s = ctx.enter_context(tc.psum_pool(name="psum_s", bufs=S_BUFS))
+        psum_acc = ctx.enter_context(tc.psum_pool(name="psum_acc", bufs=V_BUFS))
 
         warm = keep.tile([P, 1], F32, name="warm")
         ones = keep.tile([P, P], BF16, name="ones")
@@ -134,10 +141,10 @@ def tile_denseshift_t_kernel(tc, x, shift, sign, bias, out):
             cols = slice(g * GROUP * P, (g + 1) * GROUP * P)
             nc.vector.quantize_mx(out=x_codes[:, cols].bitcast(FP8X4), scales=x_scales[:, cols], in_=x_g[:])
 
-        def multiply(g, t, h):
+        def multiply(g, t, h, pool=psum_acc):
             rows = slice((GROUP * g + t) * P, (GROUP * g + t + 1) * P)
             cols = half(h)
-            acc = psum_acc.tile([P, HALF], F32, tag="acc", name="acc")
+            acc = pool.tile([P, HALF], F32, tag="acc", name="acc")
             nc.tensor.matmul_mx(
                 out=acc[:],
                 lhsT=x_codes[:, rows].bitcast(FP8X4),
@@ -167,8 +174,19 @@ def tile_denseshift_t_kernel(tc, x, shift, sign, bias, out):
             nc.tensor.matmul(out=spread[:], lhsT=ones[:], rhs=bias_pad[:, half(h)], start=True, stop=True)
             nc.scalar.copy(out=bias_sb[:, half(h)], in_=spread[:])
 
+        heat = psum_s.tile([P, HALF], F32, tag="acc", name="heat")
+
+        def keep_warm(source, cols, times):
+            first = cols.start * PACK
+            for i in range(times):
+                nc.tensor.matmul(
+                    out=heat[:], lhsT=ones[:], rhs=source[:, first : first + HALF], start=True, stop=True
+                )
+
         plus_minus(half(0))
+        keep_warm(sgn_g, half(0), 4)
         plus_minus(half(1))
+        keep_warm(sgn_g, half(1), 2)
         for i in range(4):
             power(quarter(i))
         x_g = new_x_group()
@@ -176,6 +194,7 @@ def tile_denseshift_t_kernel(tc, x, shift, sign, bias, out):
             xt = transpose_pair(0, i)
             weights(quarter(i))
             copy_pair(nc.vector.tensor_copy, xt, x_g, i)
+        keep_warm(pow_g, quarter(1), 2)
         quantise_w(half(0))
         weights(quarter(2))
         quantise_x(0, x_g)
@@ -184,39 +203,49 @@ def tile_denseshift_t_kernel(tc, x, shift, sign, bias, out):
         quantise_w(quarter(3))
 
         x_next = new_x_group()
-        ahead = [transpose_pair(1, b) for b in range(2)]
-        o_sb = results.tile([P, GROUP, OUT], F32, tag="o_sb", name="o_sb")
-        firsts = [multiply(0, t, 0) for t in range(GROUP)]
-        for t in range(3):
-            add_on_gpsimd(o_sb, firsts[t], t, 0)
         for b in range(2):
-            copy_pair(nc.scalar.copy, ahead[b], x_next, b)
-        add_on_vector(o_sb, firsts[3], 3, 0)
+            copy_pair(nc.scalar.copy, transpose_pair(1, b), x_next, b)
+        keep_warm(pow_g, quarter(2), 2)
+        keep_warm(pow_g, quarter(3), 2)
+        o_sb = results.tile([P, GROUP, OUT], F32, tag="o_sb", name="o_sb")
+        done = 0
+        accs = {}
         for t in range(GROUP):
-            acc = multiply(0, t, 1)
-            add_on_vector(o_sb, acc, t, 1)
-            if t == 1:
+            accs[t, 0] = multiply(0, t, 0, psum_s if t in S0 else psum_acc)
+            if t in S0:
+                add_on_gpsimd(o_sb, accs[t, 0], t, 0)
+        for t, h in V0:
+            if h == 1:
+                accs[t, h] = multiply(0, t, h)
+            if done == Q0:
                 quantise_x(1, x_next)
-            if t < 2:
-                store(o_sb, 0, t, t + 1)
-        store(o_sb, 0, 2, 4)
+            add_on_vector(o_sb, accs[t, h], t, h)
+            done += 1
+            if h == 1:
+                for first, last in STORE_CUTS[0]:
+                    if t == last - 1:
+                        store(o_sb, 0, first, last)
 
         for g in range(1, GROUPS):
-            x_next = None
-            if g + 1 < GROUPS:
-                x_next = new_x_group()
-                for b in range(2):
-                    copy_pair(nc.scalar.copy, transpose_pair(g + 1, b), x_next, b)
+            x_next = new_x_group() if g + 1 < GROUPS else None
             o_sb = results.tile([P, GROUP, OUT], F32, tag="o_sb", name="o_sb")
-            for j in range(2 * GROUP):
+            for j in S_BANKS:
                 t, h = divmod(j, 2)
-                acc = multiply(g, t, h)
-                if j in SCALAR_SHARE[g]:
-                    add_on_gpsimd(o_sb, acc, t, h)
+                add_on_gpsimd(o_sb, multiply(g, t, h, psum_s), t, h)
+            done = 0
+            for j in range(2 * GROUP):
+                if j in S_BANKS:
+                    pass
                 else:
+                    if done == T_AFTER and x_next is not None:
+                        for b in range(2):
+                            copy_pair(nc.scalar.copy, transpose_pair(g + 1, b), x_next, b)
+                    t, h = divmod(j, 2)
+                    acc = multiply(g, t, h)
                     add_on_vector(o_sb, acc, t, h)
-                if j == QUANT_AFTER and x_next is not None:
-                    quantise_x(g + 1, x_next)
+                    done += 1
+                    if done == QUANT_AFTER and x_next is not None:
+                        quantise_x(g + 1, x_next)
                 for first, last in STORE_CUTS[g]:
                     if j == 2 * last - 1:
                         store(o_sb, g, first, last)

@@ -22,17 +22,13 @@ WORDS = K // 2
 FLOPS = 2 * BATCH * K * OUT
 LN2 = 0.6931471805599453
 
-QUARTER = 256
 X_CHUNKS = ((0, 4), (4, 8), (8, 16), (16, 24), (24, 32))
-STORE_CUTS = (((0, 1), (1, 2), (2, 4)),) + (((0, 2), (2, 4)),) * (GROUPS - 1)
+AHEAD = 1
+SHARE = (0, 4)
 QUANT_AFTER = 3
-S_BANKS = (0, 1)
-T_AFTER = 2
-S_BUFS = 2
-S0 = (2, 3)
-V0 = ((0, 0), (0, 1), (1, 0), (1, 1), (2, 1), (3, 1))
-Q0 = 1
-V_BUFS = 4
+T_BEFORE = 3
+FIRST_SHARE_1 = ()
+STORE_CUTS = ((0, 2), (2, 4))
 OUT_BUFS = 5
 
 
@@ -44,8 +40,7 @@ def tile_denseshift_t_kernel(tc, x, shift, sign, bias, out):
         stage = ctx.enter_context(tc.tile_pool(name="stage", bufs=3))
         results = ctx.enter_context(tc.tile_pool(name="results", bufs=OUT_BUFS))
         psum_t = ctx.enter_context(tc.psum_pool(name="psum_t", bufs=2))
-        psum_s = ctx.enter_context(tc.psum_pool(name="psum_s", bufs=S_BUFS))
-        psum_acc = ctx.enter_context(tc.psum_pool(name="psum_acc", bufs=V_BUFS))
+        psum_acc = ctx.enter_context(tc.psum_pool(name="psum_acc", bufs=6))
 
         warm = keep.tile([P, 1], F32, name="warm")
         ones = keep.tile([P, P], BF16, name="ones")
@@ -53,8 +48,12 @@ def tile_denseshift_t_kernel(tc, x, shift, sign, bias, out):
         bias_pad = keep.tile([P, OUT], BF16, name="bias_pad")
         bias_sb = keep.tile([P, OUT], F32, name="bias_sb")
         x_sb = keep.tile([P, TILES * K], BF16, name="x_sb")
-        shift_sb = keep.tile([P, PACK * OUT], BF16, name="shift_sb")
-        sign_sb = keep.tile([P, PACK * OUT], BF16, name="sign_sb")
+        shift_0 = keep.tile([P, PACK * HALF], BF16, name="shift_0")
+        shift_1 = keep.tile([P, PACK * HALF], BF16, name="shift_1")
+        sign_0 = keep.tile([P, PACK * HALF], BF16, name="sign_0")
+        sign_1 = keep.tile([P, PACK * HALF], BF16, name="sign_1")
+        shift_sb = (shift_0, shift_1)
+        sign_sb = (sign_0, sign_1)
         pow_g = keep.tile([P, OUT * PACK], BF16, name="pow_g")
         sgn_g = keep.tile([P, OUT * PACK], BF16, name="sgn_g")
         w_g = keep.tile([P, OUT * PACK], BF16, name="w_g", align_bytes=64)
@@ -68,21 +67,35 @@ def tile_denseshift_t_kernel(tc, x, shift, sign, bias, out):
         nc.vector.memset(warm[:], 0.0)
         make_identity(nc, ident[:])
 
-        for dst, src in ((sign_sb, sign), (shift_sb, shift)):
-            nc.sync.dma_start(out=dst[:], in_=src.rearrange("(q t) o -> q (t o)", t=PACK))
-            if dst is sign_sb:
-                nc.sync.dma_start(out=bias_pad[0:1, :], in_=bias)
+        def half(h):
+            return slice(h * HALF, (h + 1) * HALF)
+
+        def load_half(dst, src, h):
+            nc.sync.dma_start(
+                out=dst[h][:].rearrange("q (t o) -> q t o", t=PACK),
+                in_=src.rearrange("(q t) o -> q t o", t=PACK)[:, :, half(h)],
+            )
+
         x_rows = x.rearrange("(p i) k -> p (i k)", i=TILES)
-        for first, last in X_CHUNKS:
+
+        def load_x(first, last):
             nc.sync.dma_start(out=x_sb[:, first * K : last * K], in_=x_rows[:, first * K : last * K])
+
+        load_half(shift_sb, shift, 0)
+        load_half(sign_sb, sign, 0)
+        nc.sync.dma_start(out=bias_pad[0:1, :], in_=bias)
+        load_x(*X_CHUNKS[0])
+        load_half(shift_sb, shift, 1)
+        load_half(sign_sb, sign, 1)
+        for first, last in X_CHUNKS[1:]:
+            load_x(first, last)
         x_words = x_sb[:].bitcast(F32)
         out_rows = out.rearrange("(p i) o -> p i o", i=TILES)
 
         nc.scalar.activation(out=warm[:], in_=warm[:], func=ACT.Exp)
 
-        def rows_view(t, cols):
-            by_row = t[:].rearrange("q (t o) -> q t o", t=PACK)[:, :, cols]
-            return by_row.rearrange("q t (c i) -> q c t i", i=4)
+        def rows_view(t):
+            return t[:].rearrange("q (t c i) -> q c t i", t=PACK, i=4)
 
         def grouped(cols):
             return slice(cols.start * PACK, cols.stop * PACK)
@@ -90,20 +103,14 @@ def tile_denseshift_t_kernel(tc, x, shift, sign, bias, out):
         def grouped_view(t, cols):
             return t[:, grouped(cols)].rearrange("q (c i t) -> q c t i", i=4, t=PACK)
 
-        def half(h):
-            return slice(h * HALF, (h + 1) * HALF)
-
-        def quarter(i):
-            return slice(i * QUARTER, (i + 1) * QUARTER)
-
-        def power(cols):
+        def power(h):
             nc.scalar.activation(
-                out=grouped_view(pow_g, cols), in_=rows_view(shift_sb, cols), func=ACT.Exp, scale=LN2
+                out=grouped_view(pow_g, half(h)), in_=rows_view(shift_sb[h]), func=ACT.Exp, scale=LN2
             )
 
-        def plus_minus(cols):
+        def plus_minus(h):
             nc.vector.tensor_scalar(
-                out=grouped_view(sgn_g, cols), in0=rows_view(sign_sb, cols),
+                out=grouped_view(sgn_g, half(h)), in0=rows_view(sign_sb[h]),
                 scalar1=-2.0, scalar2=1.0, op0=ALU.mult, op1=ALU.add,
             )
 
@@ -156,96 +163,90 @@ def tile_denseshift_t_kernel(tc, x, shift, sign, bias, out):
             )
             return acc
 
-        def add_on_vector(o_sb, acc, t, h):
-            nc.vector.tensor_tensor(out=o_sb[:, t, half(h)], in0=acc[:], in1=bias_sb[:, half(h)], op=ALU.add)
+        def add_on_vector(part, acc, h):
+            nc.vector.tensor_tensor(out=part, in0=acc[:], in1=bias_sb[:, half(h)], op=ALU.add)
 
-        def add_on_gpsimd(o_sb, acc, t, h):
-            part = o_sb[:, t, half(h)]
+        def add_on_gpsimd(part, acc, h):
             nc.scalar.copy(out=part, in_=acc[:])
             nc.gpsimd.tensor_tensor(out=part, in0=part, in1=bias_sb[:, half(h)], op=ALU.add)
 
-        def store(o_sb, g, first, last):
-            nc.sync.dma_start(
-                out=out_rows[:, GROUP * g + first : GROUP * g + last, :], in_=o_sb[:, first:last, :]
-            )
+        def store(part, g, first, last, cols=slice(0, OUT)):
+            nc.sync.dma_start(out=out_rows[:, GROUP * g + first : GROUP * g + last, cols], in_=part)
 
-        for h in range(2):
-            spread = psum_acc.tile([P, HALF], F32, tag="acc", name="acc")
-            nc.tensor.matmul(out=spread[:], lhsT=ones[:], rhs=bias_pad[:, half(h)], start=True, stop=True)
-            nc.scalar.copy(out=bias_sb[:, half(h)], in_=spread[:])
+        x_ready = {}
 
-        heat = psum_s.tile([P, HALF], F32, tag="acc", name="heat")
+        def prepare_x(g):
+            x_ready[g] = new_x_group()
+            for b in range(2):
+                copy_pair(nc.scalar.copy, transpose_pair(g, b), x_ready[g], b)
 
-        def keep_warm(source, cols, times):
-            first = cols.start * PACK
+        heat = psum_acc.tile([P, HALF], F32, tag="acc", name="heat")
+
+        def keep_warm(source, first, times):
             for i in range(times):
                 nc.tensor.matmul(
                     out=heat[:], lhsT=ones[:], rhs=source[:, first : first + HALF], start=True, stop=True
                 )
 
-        plus_minus(half(0))
-        keep_warm(sgn_g, half(0), 4)
-        plus_minus(half(1))
-        keep_warm(sgn_g, half(1), 2)
-        for i in range(4):
-            power(quarter(i))
-        x_g = new_x_group()
-        for i in range(2):
-            xt = transpose_pair(0, i)
-            weights(quarter(i))
-            copy_pair(nc.vector.tensor_copy, xt, x_g, i)
-        keep_warm(pow_g, quarter(1), 2)
-        quantise_w(half(0))
-        weights(quarter(2))
-        quantise_x(0, x_g)
-        weights(quarter(3))
-        quantise_w(quarter(2))
-        quantise_w(quarter(3))
+        o_0 = keep.tile([P, GROUP, HALF], F32, name="o_0")
+        o_1 = keep.tile([P, GROUP, HALF], F32, name="o_1")
 
-        x_next = new_x_group()
-        for b in range(2):
-            copy_pair(nc.scalar.copy, transpose_pair(1, b), x_next, b)
-        keep_warm(pow_g, quarter(2), 2)
-        keep_warm(pow_g, quarter(3), 2)
-        o_sb = results.tile([P, GROUP, OUT], F32, tag="o_sb", name="o_sb")
-        done = 0
+        def bank(part, g, t, h, on_gpsimd):
+            acc = multiply(g, t, h)
+            if on_gpsimd:
+                add_on_gpsimd(part, acc, h)
+            else:
+                add_on_vector(part, acc, h)
+
+        keep_warm(shift_0, 0, 3)
+        power(0)
+        plus_minus(0)
+        for h in range(2):
+            spread = psum_acc.tile([P, HALF], F32, tag="acc", name="acc")
+            nc.tensor.matmul(out=spread[:], lhsT=ones[:], rhs=bias_pad[:, half(h)], start=True, stop=True)
+            nc.scalar.copy(out=bias_sb[:, half(h)], in_=spread[:])
+        weights(half(0))
+        x_ready[0] = new_x_group()
+        xts = [transpose_pair(0, b) for b in range(2)]
+        keep_warm(w_g, 0, 3)
+        copy_pair(nc.vector.tensor_copy, xts[0], x_ready[0], 0)
+        quantise_w(half(0))
+        copy_pair(nc.scalar.copy, xts[1], x_ready[0], 1)
+        power(1)
+        quantise_x(0, x_ready[0])
+        plus_minus(1)
         accs = {}
         for t in range(GROUP):
-            accs[t, 0] = multiply(0, t, 0, psum_s if t in S0 else psum_acc)
-            if t in S0:
-                add_on_gpsimd(o_sb, accs[t, 0], t, 0)
-        for t, h in V0:
-            if h == 1:
-                accs[t, h] = multiply(0, t, h)
-            if done == Q0:
-                quantise_x(1, x_next)
-            add_on_vector(o_sb, accs[t, h], t, h)
-            done += 1
-            if h == 1:
-                for first, last in STORE_CUTS[0]:
-                    if t == last - 1:
-                        store(o_sb, 0, first, last)
+            accs[t] = multiply(0, t, 0)
+        prepare_x(1)
+        for t in ():
+            add_on_gpsimd(o_0[:, t, :], accs[t], 0)
+        add_on_vector(o_0[:, 0, :], accs[0], 0)
+        weights(half(1))
+        add_on_vector(o_0[:, 1, :], accs[1], 0)
+        store(o_0[:, 0:2, :], 0, 0, 2, half(0))
+        quantise_w(half(1))
+        for t in (2, 3):
+            if t not in ():
+                add_on_vector(o_0[:, t, :], accs[t], 0)
+        store(o_0[:, 2:4, :], 0, 2, 4, half(0))
+        quantise_x(1, x_ready[1])
+        for t in range(GROUP):
+            bank(o_1[:, t, :], 0, t, 1, t in FIRST_SHARE_1)
+            if t == 1:
+                store(o_1[:, 0:2, :], 0, 0, 2, half(1))
+        store(o_1[:, 2:4, :], 0, 2, 4, half(1))
 
         for g in range(1, GROUPS):
-            x_next = new_x_group() if g + 1 < GROUPS else None
             o_sb = results.tile([P, GROUP, OUT], F32, tag="o_sb", name="o_sb")
-            for j in S_BANKS:
-                t, h = divmod(j, 2)
-                add_on_gpsimd(o_sb, multiply(g, t, h, psum_s), t, h)
-            done = 0
+            more = g + AHEAD < GROUPS
             for j in range(2 * GROUP):
-                if j in S_BANKS:
-                    pass
-                else:
-                    if done == T_AFTER and x_next is not None:
-                        for b in range(2):
-                            copy_pair(nc.scalar.copy, transpose_pair(g + 1, b), x_next, b)
-                    t, h = divmod(j, 2)
-                    acc = multiply(g, t, h)
-                    add_on_vector(o_sb, acc, t, h)
-                    done += 1
-                    if done == QUANT_AFTER and x_next is not None:
-                        quantise_x(g + 1, x_next)
-                for first, last in STORE_CUTS[g]:
+                t, h = divmod(j, 2)
+                if j == T_BEFORE and more:
+                    prepare_x(g + AHEAD)
+                bank(o_sb[:, t, half(h)], g, t, h, j in SHARE)
+                if j == QUANT_AFTER and more:
+                    quantise_x(g + AHEAD, x_ready[g + AHEAD])
+                for first, last in STORE_CUTS:
                     if j == 2 * last - 1:
-                        store(o_sb, g, first, last)
+                        store(o_sb[:, first:last, :], g, first, last)

@@ -22,13 +22,13 @@ WORDS = K // 2
 FLOPS = 2 * BATCH * K * OUT
 LN2 = 0.6931471805599453
 
-X_CHUNKS = ((0, 4), (4, 8), (8, 16), (16, 24), (24, 32))
-AHEAD = 1
+X_CHUNKS = ((0, 4), (4, 12), (12, 32))
 SHARE = (0, 4)
 QUANT_AFTER = 3
 T_BEFORE = 3
-FIRST_SHARE_1 = ()
-STORE_CUTS = ((0, 2), (2, 4))
+FIRST_SHARE_1 = (2,)
+HALVES = ((0, 2), (2, 4))
+STORE_CUTS = (HALVES,) * 5 + (((0, 4),),) * 2 + (HALVES,)
 OUT_BUFS = 5
 
 
@@ -209,7 +209,7 @@ def tile_denseshift_t_kernel(tc, x, shift, sign, bias, out):
         x_ready[0] = new_x_group()
         xts = [transpose_pair(0, b) for b in range(2)]
         keep_warm(w_g, 0, 3)
-        copy_pair(nc.vector.tensor_copy, xts[0], x_ready[0], 0)
+        copy_pair(nc.scalar.copy, xts[0], x_ready[0], 0)
         quantise_w(half(0))
         copy_pair(nc.scalar.copy, xts[1], x_ready[0], 1)
         power(1)
@@ -219,16 +219,13 @@ def tile_denseshift_t_kernel(tc, x, shift, sign, bias, out):
         for t in range(GROUP):
             accs[t] = multiply(0, t, 0)
         prepare_x(1)
-        for t in ():
-            add_on_gpsimd(o_0[:, t, :], accs[t], 0)
         add_on_vector(o_0[:, 0, :], accs[0], 0)
         weights(half(1))
         add_on_vector(o_0[:, 1, :], accs[1], 0)
         store(o_0[:, 0:2, :], 0, 0, 2, half(0))
         quantise_w(half(1))
         for t in (2, 3):
-            if t not in ():
-                add_on_vector(o_0[:, t, :], accs[t], 0)
+            add_on_vector(o_0[:, t, :], accs[t], 0)
         store(o_0[:, 2:4, :], 0, 2, 4, half(0))
         quantise_x(1, x_ready[1])
         for t in range(GROUP):
@@ -239,14 +236,14 @@ def tile_denseshift_t_kernel(tc, x, shift, sign, bias, out):
 
         for g in range(1, GROUPS):
             o_sb = results.tile([P, GROUP, OUT], F32, tag="o_sb", name="o_sb")
-            more = g + AHEAD < GROUPS
+            more = g + 1 < GROUPS
             for j in range(2 * GROUP):
                 t, h = divmod(j, 2)
                 if j == T_BEFORE and more:
-                    prepare_x(g + AHEAD)
+                    prepare_x(g + 1)
                 bank(o_sb[:, t, half(h)], g, t, h, j in SHARE)
                 if j == QUANT_AFTER and more:
-                    quantise_x(g + AHEAD, x_ready[g + AHEAD])
-                for first, last in STORE_CUTS:
+                    quantise_x(g + 1, x_ready[g + 1])
+                for first, last in STORE_CUTS[g]:
                     if j == 2 * last - 1:
                         store(o_sb[:, first:last, :], g, first, last)

@@ -180,14 +180,6 @@ def tile_denseshift_t_kernel(tc, x, shift, sign, bias, out):
             for b in range(2):
                 copy_pair(nc.scalar.copy, transpose_pair(g, b), x_ready[g], b)
 
-        heat = psum_acc.tile([P, HALF], F32, tag="acc", name="heat")
-
-        def keep_warm(source, first, times):
-            for i in range(times):
-                nc.tensor.matmul(
-                    out=heat[:], lhsT=ones[:], rhs=source[:, first : first + HALF], start=True, stop=True
-                )
-
         o_0 = keep.tile([P, GROUP, HALF], F32, name="o_0")
         o_1 = keep.tile([P, GROUP, HALF], F32, name="o_1")
 
@@ -198,7 +190,6 @@ def tile_denseshift_t_kernel(tc, x, shift, sign, bias, out):
             else:
                 add_on_vector(part, acc, h)
 
-        keep_warm(shift_0, 0, 3)
         power(0)
         plus_minus(0)
         for h in range(2):
@@ -208,7 +199,6 @@ def tile_denseshift_t_kernel(tc, x, shift, sign, bias, out):
         weights(half(0))
         x_ready[0] = new_x_group()
         xts = [transpose_pair(0, b) for b in range(2)]
-        keep_warm(w_g, 0, 3)
         copy_pair(nc.scalar.copy, xts[0], x_ready[0], 0)
         quantise_w(half(0))
         copy_pair(nc.scalar.copy, xts[1], x_ready[0], 1)

from contextlib import ExitStack

import concourse.mybir as mybir
from concourse.masks import make_identity

F32 = mybir.dt.float32
BF16 = mybir.dt.bfloat16
U32 = mybir.dt.uint32
U8 = mybir.dt.uint8
FP8X4 = mybir.dt.float8_e4m3fn_x4
ALU = mybir.AluOpType
ACT = mybir.ActivationFunctionType

P = 128
BATCH, K, OUT = 4096, 512, 1024
PACK = 4
TILES = BATCH // P
GROUP = 4
GROUPS = TILES // GROUP
HALF = 512
WORDS = K // 2
FLOPS = 2 * BATCH * K * OUT
LN2 = 0.6931471805599453

X_CHUNKS = ((0, 4), (4, 12), (12, 32))
SHARE = (0, 4)
QUANT_AFTER = 3
T_BEFORE = 3
FIRST_SHARE_1 = (2,)
HALVES = ((0, 2), (2, 4))
STORE_CUTS = (HALVES,) * 5 + (((0, 4),),) * 2 + (HALVES,)
OUT_BUFS = 5


def tile_denseshift_t_kernel(tc, x, shift, sign, bias, out):
    nc = tc.nc
    with ExitStack() as ctx:
        ctx.enter_context(tc.manual_schedule())
        keep = ctx.enter_context(tc.tile_pool(name="keep", bufs=1))
        stage = ctx.enter_context(tc.tile_pool(name="stage", bufs=3))
        results = ctx.enter_context(tc.tile_pool(name="results", bufs=OUT_BUFS))
        psum_t = ctx.enter_context(tc.psum_pool(name="psum_t", bufs=2))
        psum_acc = ctx.enter_context(tc.psum_pool(name="psum_acc", bufs=6))

        warm = keep.tile([P, 1], F32, name="warm")
        ones = keep.tile([P, P], BF16, name="ones")
        ident = keep.tile([P, P], F32, name="ident")
        bias_pad = keep.tile([P, OUT], BF16, name="bias_pad")
        bias_sb = keep.tile([P, OUT], F32, name="bias_sb")
        x_sb = keep.tile([P, TILES * K], BF16, name="x_sb")
        shift_0 = keep.tile([P, PACK * HALF], BF16, name="shift_0")
        shift_1 = keep.tile([P, PACK * HALF], BF16, name="shift_1")
        sign_0 = keep.tile([P, PACK * HALF], BF16, name="sign_0")
        sign_1 = keep.tile([P, PACK * HALF], BF16, name="sign_1")
        shift_sb = (shift_0, shift_1)
        sign_sb = (sign_0, sign_1)
        pow_g = keep.tile([P, OUT * PACK], BF16, name="pow_g")
        sgn_g = keep.tile([P, OUT * PACK], BF16, name="sgn_g")
        w_g = keep.tile([P, OUT * PACK], BF16, name="w_g", align_bytes=64)
        w_codes = keep.tile([P, OUT], U32, name="w_codes", align_bytes=64)
        w_scales = keep.tile([P, OUT], U8, name="w_scales", align_bytes=64)
        x_codes = keep.tile([P, BATCH], U32, name="x_codes", align_bytes=64)
        x_scales = keep.tile([P, BATCH], U8, name="x_scales", align_bytes=64)

        nc.vector.memset(bias_pad[:], 0.0)
        nc.vector.memset(ones[:], 1.0)
        nc.vector.memset(warm[:], 0.0)
        make_identity(nc, ident[:])

        def half(h):
            return slice(h * HALF, (h + 1) * HALF)

        def load_half(dst, src, h):
            nc.sync.dma_start(
                out=dst[h][:].rearrange("q (t o) -> q t o", t=PACK),
                in_=src.rearrange("(q t) o -> q t o", t=PACK)[:, :, half(h)],
            )

        x_rows = x.rearrange("(p i) k -> p (i k)", i=TILES)

        def load_x(first, last):
            nc.sync.dma_start(out=x_sb[:, first * K : last * K], in_=x_rows[:, first * K : last * K])

        load_half(shift_sb, shift, 0)
        load_half(sign_sb, sign, 0)
        nc.sync.dma_start(out=bias_pad[0:1, :], in_=bias)
        load_x(*X_CHUNKS[0])
        load_half(shift_sb, shift, 1)
        load_half(sign_sb, sign, 1)
        for first, last in X_CHUNKS[1:]:
            load_x(first, last)
        x_words = x_sb[:].bitcast(F32)
        out_rows = out.rearrange("(p i) o -> p i o", i=TILES)

        nc.scalar.activation(out=warm[:], in_=warm[:], func=ACT.Exp)

        def rows_view(t):
            return t[:].rearrange("q (t c i) -> q c t i", t=PACK, i=4)

        def grouped(cols):
            return slice(cols.start * PACK, cols.stop * PACK)

        def grouped_view(t, cols):
            return t[:, grouped(cols)].rearrange("q (c i t) -> q c t i", i=4, t=PACK)

        def power(h):
            nc.scalar.activation(
                out=grouped_view(pow_g, half(h)), in_=rows_view(shift_sb[h]), func=ACT.Exp, scale=LN2
            )

        def plus_minus(h):
            nc.vector.tensor_scalar(
                out=grouped_view(sgn_g, half(h)), in0=rows_view(sign_sb[h]),
                scalar1=-2.0, scalar2=1.0, op0=ALU.mult, op1=ALU.add,
            )

        def weights(cols):
            part = grouped(cols)
            nc.vector.tensor_tensor(out=w_g[:, part], in0=pow_g[:, part], in1=sgn_g[:, part], op=ALU.mult)

        def quantise_w(cols):
            nc.vector.quantize_mx(
                out=w_codes[:, cols].bitcast(FP8X4), scales=w_scales[:, cols], in_=w_g[:, grouped(cols)]
            )

        def new_x_group():
            return stage.tile([P, GROUP * K], BF16, tag="x_g", name="x_g", align_bytes=64)

        def transpose_pair(g, b):
            xt = psum_t.tile([P, 4, P], F32, tag="xt", name="xt")
            for pair in range(2):
                i = GROUP * g + 2 * b + pair
                for u in range(2):
                    every_second = slice(WORDS * i + u, WORDS * (i + 1), 2)
                    nc.tensor.transpose(xt[:, 2 * pair + u, :], x_words[:, every_second], ident[:])
            return xt

        def copy_pair(copy, xt, x_g, b):
            x_g_words = x_g[:].bitcast(F32)
            copy(
                out=x_g_words[:, 2 * WORDS * b : 2 * WORDS * (b + 1)].rearrange(
                    "q (pair r u) -> q pair r u", pair=2, u=2
                ),
                in_=xt[:].rearrange("q (pair u) r -> q pair r u", u=2),
            )

        def quantise_x(g, x_g):
            cols = slice(g * GROUP * P, (g + 1) * GROUP * P)
            nc.vector.quantize_mx(out=x_codes[:, cols].bitcast(FP8X4), scales=x_scales[:, cols], in_=x_g[:])

        def multiply(g, t, h, pool=psum_acc):
            rows = slice((GROUP * g + t) * P, (GROUP * g + t + 1) * P)
            cols = half(h)
            acc = pool.tile([P, HALF], F32, tag="acc", name="acc")
            nc.tensor.matmul_mx(
                out=acc[:],
                lhsT=x_codes[:, rows].bitcast(FP8X4),
                lhsT_scale=x_scales[:, rows],
                rhs=w_codes[:, cols].bitcast(FP8X4),
                rhs_scale=w_scales[:, cols],
                start=True,
                stop=True,
            )
            return acc

        def add_on_vector(part, acc, h):
            nc.vector.tensor_tensor(out=part, in0=acc[:], in1=bias_sb[:, half(h)], op=ALU.add)

        def add_on_gpsimd(part, acc, h):
            nc.scalar.copy(out=part, in_=acc[:])
            nc.gpsimd.tensor_tensor(out=part, in0=part, in1=bias_sb[:, half(h)], op=ALU.add)

        def store(part, g, first, last, cols=slice(0, OUT)):
            nc.sync.dma_start(out=out_rows[:, GROUP * g + first : GROUP * g + last, cols], in_=part)

        x_ready = {}

        def prepare_x(g):
            x_ready[g] = new_x_group()
            for b in range(2):
                copy_pair(nc.scalar.copy, transpose_pair(g, b), x_ready[g], b)

        o_0 = keep.tile([P, GROUP, HALF], F32, name="o_0")
        o_1 = keep.tile([P, GROUP, HALF], F32, name="o_1")

        def bank(part, g, t, h, on_gpsimd):
            acc = multiply(g, t, h)
            if on_gpsimd:
                add_on_gpsimd(part, acc, h)
            else:
                add_on_vector(part, acc, h)

        power(0)
        plus_minus(0)
        for h in range(2):
            spread = psum_acc.tile([P, HALF], F32, tag="acc", name="acc")
            nc.tensor.matmul(out=spread[:], lhsT=ones[:], rhs=bias_pad[:, half(h)], start=True, stop=True)
            nc.scalar.copy(out=bias_sb[:, half(h)], in_=spread[:])
        weights(half(0))
        x_ready[0] = new_x_group()
        xts = [transpose_pair(0, b) for b in range(2)]
        copy_pair(nc.scalar.copy, xts[0], x_ready[0], 0)
        quantise_w(half(0))
        copy_pair(nc.scalar.copy, xts[1], x_ready[0], 1)
        power(1)
        quantise_x(0, x_ready[0])
        plus_minus(1)
        accs = {}
        for t in range(GROUP):
            accs[t] = multiply(0, t, 0)
        prepare_x(1)
        add_on_vector(o_0[:, 0, :], accs[0], 0)
        weights(half(1))
        add_on_vector(o_0[:, 1, :], accs[1], 0)
        store(o_0[:, 0:2, :], 0, 0, 2, half(0))
        quantise_w(half(1))
        for t in (2, 3):
            add_on_vector(o_0[:, t, :], accs[t], 0)
        store(o_0[:, 2:4, :], 0, 2, 4, half(0))
        quantise_x(1, x_ready[1])
        for t in range(GROUP):
            bank(o_1[:, t, :], 0, t, 1, t in FIRST_SHARE_1)
            if t == 1:
                store(o_1[:, 0:2, :], 0, 0, 2, half(1))
        store(o_1[:, 2:4, :], 0, 2, 4, half(1))

        for g in range(1, GROUPS):
            o_sb = results.tile([P, GROUP, OUT], F32, tag="o_sb", name="o_sb")
            more = g + 1 < GROUPS
            for j in range(2 * GROUP):
                t, h = divmod(j, 2)
                if j == T_BEFORE and more:
                    prepare_x(g + 1)
                bank(o_sb[:, t, half(h)], g, t, h, j in SHARE)
                if j == QUANT_AFTER and more:
                    quantise_x(g + 1, x_ready[g + 1])
                for first, last in STORE_CUTS[g]:
                    if j == 2 * last - 1:
                        store(o_sb[:, first:last, :], g, first, last)
